import numpy as np
import ml_dtypes


def mxq(x, axis, fmt="e4m3"):
    dtype, down = {"e4m3": (ml_dtypes.float8_e4m3fn, 7), "e5m2": (ml_dtypes.float8_e5m2, 14)}[fmt]
    v = np.moveaxis(np.asarray(x, np.float32).astype(ml_dtypes.bfloat16).astype(np.float64), axis, -1)
    blocks = v.reshape(v.shape[:-1] + (-1, 32))
    amax = np.abs(blocks).max(-1, keepdims=True)
    byte = np.maximum(np.where(amax > 0, np.frexp(amax)[1] - 1 + 127, 0) - down, 1)
    scale = np.exp2(byte - 127.0)
    codes = (blocks / scale).astype(np.float32).astype(dtype).astype(np.float64)
    return np.moveaxis((codes * scale).reshape(v.shape), -1, axis)


WIDE = False


def mx_kscale(k):
    if not WIDE:
        return np.ones(k)
    levels = np.array([10, -10, 5, -5, 0])
    if k % 512:
        return np.exp2(np.random.permutation(np.resize(levels, k // 32))).repeat(32)
    a = np.empty((k // 512, 16))
    for p in range(k // 512):
        a[p, :8] = np.random.permutation(np.resize(levels, 8))
        for g in range(8):
            far = levels[np.abs(levels - a[p, g]) >= 10]
            a[p, g + 8] = far[np.random.randint(len(far))]
    return np.exp2(a.ravel()).repeat(32)


BF16 = ml_dtypes.bfloat16


def bf(x):
    return np.asarray(x, np.float32).astype(BF16)


def f64(x):
    return np.asarray(x).astype(np.float64)


B, S, D, DR = 2, 512, 1024, 1024
G = 1.4 * (D / DR) ** 0.25 / np.sqrt(D)


def draw0():
    s = mx_kscale(D)
    t = mx_kscale(DR)
    mask = (np.random.random((S, S)) < 0.5) & ~np.eye(S, dtype=bool)
    return {"q_lin": bf(np.random.standard_normal((B, S, D)) * s),
            "k_lin": bf(np.random.standard_normal((B, S, D)) * s),
            "rotation_params": bf(np.random.standard_normal((DR, D)) * G * t[:, None] / s),
            "entangle_params": bf(np.random.standard_normal((DR, D)) * G / t[:, None] / s),
            "mask": mask}


def core(q_lin, k_lin, rotation_params, entangle_params, mask):
    q = mxq(f64(q_lin), 2, "e4m3") @ mxq(f64(rotation_params), 1, "e4m3").T
    k = mxq(f64(k_lin), 2, "e4m3") @ mxq(f64(entangle_params), 1, "e4m3").T
    scores = (mxq(q, 2, "e4m3") @ mxq(k, 2, "e4m3").transpose(0, 2, 1)) / np.sqrt(D)
    scores = np.where(f64(mask) > 0.5, -np.inf, scores)
    e = np.exp(scores - scores.max(-1, keepdims=True))
    return e / e.sum(-1, keepdims=True)


def e4m3fn_bytes(y):
    return np.clip(np.asarray(y, np.float64), -448.0, 448.0).astype(np.float32).astype(ml_dtypes.float8_e4m3fn).view(np.uint8)


def e4m3fn_values(b):
    return np.asarray(b, np.uint8).view(ml_dtypes.float8_e4m3fn).astype(np.float64)


def setup_inputs():
    d = draw0()
    x0 = np.asarray(d['q_lin']).astype(np.float64)
    s = (np.max(np.abs(x0), axis=(0, 1), keepdims=True) / 448.0).astype(np.float32)
    out = {}
    for k, v in d.items():
        if k == 'q_lin':
            out['q_lin_bytes'] = e4m3fn_bytes(x0 / s.astype(np.float64))
            out['q_lin_scale'] = s
        else:
            out[k] = v
    return out


def reference(q_lin_bytes, q_lin_scale, k_lin, rotation_params, entangle_params, mask):
    return core(e4m3fn_values(q_lin_bytes) * q_lin_scale.astype(np.float64), k_lin, rotation_params, entangle_params, mask)

from contextlib import ExitStack

import concourse.mybir as mybir
from concourse.masks import make_identity

F32 = mybir.dt.float32
BF16 = mybir.dt.bfloat16
I32 = mybir.dt.int32
U32 = mybir.dt.uint32
U8 = mybir.dt.uint8
E4M3 = mybir.dt.float8_e4m3fn
E4M3X4 = mybir.dt.float8_e4m3fn_x4

ALU = mybir.AluOpType
ACT = mybir.ActivationFunctionType
AXIS = mybir.AxisListType

B, S, D = 2, 512, 1024
P = 128
PACK = 4
PASSES = D // (P * PACK)
GROUPS = D // (P * PACK)
TILES = S // P
INV_SQRT_D = 1.0 / 32.0
MASKED = -1.0e30

RUN0, RUN, MULT, LAG = 5, 2, 1, 2
WARM, HEAD_SPIN, SPIN, SPIN_N = 5, 1, 0, 512
ORDER_D = "k001 z e001 e012 e023 e034 k012 k023 k034 e102 e124 r002 q0 r024 r104 k104 m02 m24 q1"
NR0, NR1, DR = 1, 12, 3
REORDER_ON = "v"
SC1, SC2 = 2, 5
ORDER_T = "k00 e00 e01 e02 e03 k01 k02 k03 e10 e11 e12 e13 r00 r01 r03 r11 r12 q00 q01 r02 q02 k11 q03 k10 k12 q13 q12 q11 r10 r13 k13 q10"
ORDER_M = "k000 k001 k002 k102 k003 k101 k100 k103 q001 q000 q003 q002 q100 k010 q101 k011 s01 q102 s00 k012 q103 k013 s02 k110 k111 k112 s03 k113 q010 q110 q011 q111 s10 q012 q112 s11 q013 q113 s12 s13"
DQ, DP, D1, D2, D3, D4, DW = 1, 2, 0, 1, 2, 5, 5

FLOPS = 2 * (2 * B * S * D * D + B * S * S * D)


def tile_selfattention_pa_kernel(
    tc, q_lin_bytes, q_lin_scale, k_lin, rotation_params, entangle_params, mask, out
):
    nc = tc.nc

    with ExitStack() as ctx:
        keep = ctx.enter_context(tc.tile_pool(name="keep", bufs=1))
        work = ctx.enter_context(tc.tile_pool(name="work", bufs=6))
        soft = ctx.enter_context(tc.tile_pool(name="soft", bufs=3))
        psum = ctx.enter_context(tc.psum_pool(name="psum", bufs=8))

        zeros = keep.tile([P, S], BF16, name="zeros")
        nc.gpsimd.memset(zeros[:], 0.0)
        scale_rows = keep.tile([P, P], F32, name="scale_rows")
        nc.gpsimd.memset(scale_rows[:], 0.0)
        ident = keep.tile([P, P], F32, name="ident")
        make_identity(nc, ident[:])
        warm = keep.tile([P, 2], F32, name="warm")
        nc.vector.memset(warm[:], 0.0)

        ctx.enter_context(tc.manual_schedule())

        nc.scalar.activation(out=warm[:, 1:2], in_=warm[:, 0:1], func=ACT.Exp)

        def load(name, shape, dtype, src):
            t = keep.tile(shape, dtype, name=name, align_bytes=64)
            nc.sync.dma_start(out=t[:], in_=src)
            return t

        raw = {}
        q_bytes = {}
        mask_words = {}
        mask_rows = mask.bitcast(I32).rearrange("(m t) w -> m t w", t=TILES)
        for token in ORDER_D.split(" "):
            kind = token[0]
            if kind == "z":
                nc.sync.dma_start(
                    out=scale_rows[0 : D // P, :], in_=q_lin_scale.rearrange("a o (m n) -> (a o m) n", n=P)
                )
            elif kind == "q":
                b = int(token[1])
                q_bytes[b] = load("q_in_%d" % b, [P, TILES, D], U8, q_lin_bytes[b].rearrange("(m t) k -> m t k", t=TILES))
            elif kind == "m":
                lo, hi = int(token[1]), int(token[2])
                t = load("mask_%d" % lo, [P, hi - lo, 2 * S], I32, mask_rows[:, lo:hi, :])
                for j in range(lo, hi):
                    mask_words[j] = t[:, j - lo, 0 : 2 * S : 2]
            else:
                g, lo, hi = int(token[1]), int(token[2]), int(token[3])
                if kind == "k":
                    rows = k_lin[g].rearrange("(j p) k -> p j k", p=P)
                elif kind == "e":
                    rows = entangle_params.rearrange("(g m t) k -> g m t k", m=P, t=PACK)[g]
                else:
                    rows = rotation_params.rearrange("(g m t) k -> g m t k", m=P, t=PACK)[g]
                t = load("%s_raw_%d_%d" % (kind, g, lo), [P, hi - lo, D], BF16, rows[:, lo:hi, :])
                for n in range(lo, hi):
                    raw[kind, g, n] = t[:, n - lo, :]

        place = {}
        proj_started = []

        todo = []
        clock = [0]
        busy = {"v": 0.0, "s": 0.0}

        def later(delay, key, step):
            todo.append((clock[0] + delay, key, step))

        def run_todo(wanted):
            ready = [entry for entry in todo if wanted(entry)]
            for entry in ready:
                todo.remove(entry)
            for entry in ready:
                entry[2]()

        def tick():
            run_todo(lambda entry: entry[0] <= clock[0])
            clock[0] += 1

        def require(keys):
            run_todo(lambda entry: entry[1] in keys)

        def empty_bank(dst, src):
            if busy["s"] <= busy["v"]:
                busy["s"] += 0.44
                nc.scalar.copy(out=dst, in_=src)
            else:
                busy["v"] += 0.44
                nc.vector.tensor_copy(out=dst, in_=src)

        codes = {}

        def quantize(key, name, grouped, width, passes):
            c = keep.tile([P, passes, width], U32, name="codes_" + name, align_bytes=64)
            s = keep.tile([P, passes, width], U8, name="scales_" + name, align_bytes=64)
            busy["v"] += 0.03 + 0.22e-3 * 4 * passes * width
            nc.vector.quantize_mx(
                out=c[:].rearrange("p c n -> p (c n)").bitcast(E4M3X4),
                scales=s[:].rearrange("p c n -> p (c n)"),
                in_=grouped,
            )
            codes[key] = (c, s)

        def spin(bank, times):
            for n in range(times):
                nc.tensor.matmul(out=bank, lhsT=zeros[:, 0:P], rhs=zeros[:, 0:SPIN_N], start=True, stop=True)

        def turn(key):
            name = "%s_%d_%d" % key
            words = raw[key].bitcast(F32)
            if key in ordered:
                words = ordered[key]
            bank = psum.tile([P, PASSES, 2, P], F32, name="bank")
            flat = bank[:].rearrange("p c u r -> p (c u r)")[:, 0:SPIN_N]
            if not place:
                spin(flat, WARM)
            elif not proj_started:
                spin(flat, HEAD_SPIN)
            else:
                spin(flat, SPIN)
            for c in range(PASSES):
                for u in range(2):
                    if key in ordered:
                        nc.tensor.transpose(bank[:, c, u, :], words[:, c, u, :], ident[:])
                    else:
                        nc.tensor.transpose(bank[:, c, u, :], words[:, 256 * c + u : 256 * (c + 1) : 2], ident[:])
            grouped = work.tile([P, PASSES * P * PACK], BF16, name="grouped", align_bytes=64)
            empty_bank(
                grouped[:].bitcast(F32).rearrange("p (c r u) -> p c r u", c=PASSES, u=2),
                bank[:].rearrange("p c u r -> p c r u"),
            )
            later(DQ, key, lambda: quantize(key, name, grouped[:], P, PASSES))

        scale_columns = keep.tile([P, D // P], F32, name="scale_columns")
        q_scale = keep.tile([P, D], F32, name="q_scale", align_bytes=64)

        def turn_scale():
            bank = psum.tile([P, S], F32, name="bank")
            nc.tensor.transpose(bank[:, 0:P], scale_rows[:], ident[:])
            nc.vector.tensor_copy(out=scale_columns[:], in_=bank[:, 0 : D // P])

        def spread_scale():
            for half in range(2):
                bank = psum.tile([P, S], F32, name="bank")
                for m in range(4):
                    column = scale_columns[:, 4 * half + m : 4 * half + m + 1].to_broadcast([P, P])
                    nc.tensor.transpose(bank[:, P * m : P * (m + 1)], column, ident[:])
                empty_bank(q_scale[:, S * half : S * (half + 1)], bank[:])

        ordered = {}

        def reorder(key):
            t = work.tile([P, PASSES, 2, P], F32, name="ordered", align_bytes=64)
            src = raw[key].bitcast(F32).rearrange("p (c m u) -> p c u m", c=PASSES, u=2)
            if "v" in REORDER_ON:
                busy["v"] += 0.24
                nc.vector.tensor_copy(out=t[:], in_=src)
            else:
                busy["s"] += 0.46
                nc.scalar.copy(out=t[:], in_=src)
            ordered[key] = t

        def widen_q(b, j):
            x = keep.tile([P, D], BF16, name="q_raw_%d_%d" % (b, j), align_bytes=64)
            busy["v"] += 0.87
            nc.vector.tensor_tensor(out=x[:], in0=q_bytes[b][:, j, :].bitcast(E4M3), in1=q_scale[:], op=ALU.mult)
            raw["q", b, j] = x[:]

        proj = {}
        for kind in ("q", "k"):
            for b in range(B):
                for g in range(GROUPS):
                    name = "%s_%d_%d" % (kind, b, g)
                    pc = keep.tile([P, S], U32, name="pcodes_" + name, align_bytes=64)
                    ps = keep.tile([P, S], U8, name="pscales_" + name, align_bytes=64)
                    proj[kind, b, g] = (pc, ps)

        def project(w, kind, g, b, j):
            bank = psum.tile([P, PACK, P], F32, name="bank")
            proj_started.append(1)
            require([(kind, b, j)] + [(w, g, t) for t in range(PACK)])
            xc, xs = codes[kind, b, j]
            for t in range(PACK):
                wc, ws = codes[w, g, t]
                for c in range(PASSES):
                    nc.tensor.matmul_mx(
                        out=bank[:, t, :],
                        lhsT=wc[:, c, :].bitcast(E4M3X4),
                        lhsT_scale=ws[:, c, :],
                        rhs=xc[:, c, :].bitcast(E4M3X4),
                        rhs_scale=xs[:, c, :],
                        start=(c == 0),
                        stop=(c == PASSES - 1),
                    )
            grouped = work.tile([P, P * PACK], BF16, name="pgrouped", align_bytes=64)
            empty_bank(grouped[:].rearrange("p (n t) -> p n t", t=PACK), bank[:].rearrange("p t n -> p n t"))
            pc, ps = proj[kind, b, g]

            def finish():
                busy["v"] += 0.14
                nc.vector.quantize_mx(
                    out=pc[:, P * j : P * (j + 1)].bitcast(E4M3X4), scales=ps[:, P * j : P * (j + 1)], in_=grouped[:]
                )

            later(DP, (kind + "p", b, g, j), finish)

        def score(b, j):
            require([("qp", b, g, j) for g in range(GROUPS)])
            require([("kp", b, g, n) for g in range(GROUPS) for n in range(TILES)])
            bank = psum.tile([P, S], F32, name="bank")
            for g in range(GROUPS):
                qc, qs = proj["q", b, g]
                kc, ks = proj["k", b, g]
                nc.tensor.matmul_mx(
                    out=bank[:],
                    lhsT=qc[:, P * j : P * (j + 1)].bitcast(E4M3X4),
                    lhsT_scale=qs[:, P * j : P * (j + 1)],
                    rhs=kc[:].bitcast(E4M3X4),
                    rhs_scale=ks[:],
                    start=(g == 0),
                    stop=(g == GROUPS - 1),
                )
            masked = soft.tile([P, S], F32, name="masked")
            top = soft.tile([P, 1], F32, name="top")
            shift = soft.tile([P, 1], F32, name="shift")
            total = soft.tile([P, 1], F32, name="total")
            inverse = soft.tile([P, 1], F32, name="inverse")
            e = soft.tile([P, S], F32, name="e")
            weights = soft.tile([P, S], F32, name="weights")
            busy["v"] += 1.4
            busy["s"] += 0.6

            def cover():
                nc.vector.scalar_tensor_tensor(
                    out=masked[:],
                    in0=mask_words[j],
                    scalar=MASKED,
                    in1=bank[:],
                    op0=ALU.mult,
                    op1=ALU.add,
                )

            def largest():
                nc.vector.tensor_reduce(out=top[:], in_=masked[:], axis=AXIS.X, op=ALU.max)

            def exponent():
                nc.scalar.mul(out=shift[:], in_=top[:], mul=-INV_SQRT_D)
                nc.scalar.activation(
                    out=e[:], in_=masked[:], func=ACT.Exp, bias=shift[:], scale=INV_SQRT_D, accum_out=total[:]
                )

            def normalise():
                nc.vector.reciprocal(out=inverse[:], in_=total[:])
                nc.vector.tensor_scalar(out=weights[:], in0=e[:], scalar1=inverse[:], scalar2=None, op0=ALU.mult)
                nc.sync.dma_start(out=out[b].rearrange("(m t) n -> t m n", t=TILES)[j], in_=weights[:])

            later(D1, ("s1", b, j), cover)
            later(D2, ("s2", b, j), largest)
            later(D3, ("s3", b, j), exponent)
            later(D4, ("s4", b, j), normalise)

        turns = [(token[0], int(token[1]), int(token[2])) for token in ORDER_T.split(" ")]
        products = [(token[0],) + tuple(int(c) for c in token[1:]) for token in ORDER_M.split(" ")]

        weights_of = {"k": "e", "q": "r"}
        count = 0
        done = 0
        turned = 0
        while done < len(products):
            run = RUN0 if turned == 0 else RUN
            for n in range(turned, min(turned + run, len(turns))):
                key = turns[n]
                for ahead in turns[n : n + DW]:
                    if ahead[0] == "q" and ahead not in raw:
                        widen_q(ahead[1], ahead[2])
                for ahead in turns[n : n + DR]:
                    place_in_turns = turns.index(ahead)
                    if ahead in raw and ahead not in ordered and NR0 <= place_in_turns < NR1:
                        reorder(ahead)
                if n == SC1:
                    turn_scale()
                if n == SC2:
                    spread_scale()
                turn(key)
                place[key] = count
                count += 1
                tick()
            turned = min(turned + run, len(turns))
            here = 0
            while done < len(products) and (here < MULT or turned == len(turns)):
                unit = products[done]
                if unit[0] != "s":
                    kind, g, b, j = unit
                    needs = [(kind, b, j)] + [(weights_of[kind], g, t) for t in range(PACK)]
                    if turned < len(turns) and any(n not in place or count - place[n] < LAG for n in needs):
                        break
                    project(weights_of[kind], kind, g, b, j)
                else:
                    score(unit[1], unit[2])
                count += 1
                done += 1
                here += 1
                tick()
        while todo:
            tick()
